import numpy as np
import ml_dtypes


def mxq(x, axis, fmt="e4m3"):
    dtype, down = {"e4m3": (ml_dtypes.float8_e4m3fn, 7), "e5m2": (ml_dtypes.float8_e5m2, 14)}[fmt]
    v = np.moveaxis(np.asarray(x, np.float32).astype(ml_dtypes.bfloat16).astype(np.float64), axis, -1)
    blocks = v.reshape(v.shape[:-1] + (-1, 32))
    amax = np.abs(blocks).max(-1, keepdims=True)
    byte = np.maximum(np.where(amax > 0, np.frexp(amax)[1] - 1 + 127, 0) - down, 1)
    scale = np.exp2(byte - 127.0)
    codes = (blocks / scale).astype(np.float32).astype(dtype).astype(np.float64)
    return np.moveaxis((codes * scale).reshape(v.shape), -1, axis)


WIDE = False


def mx_kscale(k):
    if not WIDE:
        return np.ones(k)
    levels = np.array([10, -10, 5, -5, 0])
    a = np.random.permutation(np.resize(levels, k // 512 * 4)).reshape(k // 512, 4)
    idx = np.arange(k)
    return np.exp2(a[idx // 512, idx % 128 // 32])


BF16 = ml_dtypes.bfloat16


def bf(x):
    return np.asarray(x, np.float32).astype(BF16)


def f64(x):
    return np.asarray(x).astype(np.float64)


B, N, C, H, D, S = 4, 1024, 512, 4, 128, 128
E = H * D


def setup_inputs():
    s = mx_kscale(C)
    return {"x": bf(np.random.standard_normal((B, N, C)) * s),
            "x_mid": bf(np.random.standard_normal((B, N, H, D))),
            "Wfx": bf(np.random.standard_normal((C, E)) / np.sqrt(C) / s[:, None]),
            "bfx": bf(np.random.standard_normal(E) * 0.2),
            "Wslice": bf(np.random.standard_normal((D, S)) * 2.0 / np.sqrt(D)),
            "bslice": bf(np.random.standard_normal(S) * 2.0),
            "temp": bf(np.random.uniform(0.5, 1.5, (1, 1, H, 1)))}


def reference(x, x_mid, Wfx, bfx, Wslice, bslice, temp):
    fx = (mxq(f64(x), 2, "e4m3") @ mxq(f64(Wfx), 0, "e4m3")) + f64(bfx)
    proj = f64(x_mid) @ f64(Wslice) + f64(bslice)
    z = proj / f64(temp)
    e = np.exp(z - z.max(-1, keepdims=True))
    slice_weights = e / e.sum(-1, keepdims=True)
    slice_norm = slice_weights.sum(1) + 0.01
    normed = slice_weights / slice_norm[:, None, :, :]
    a = normed.transpose(0, 2, 3, 1)
    f = fx.reshape(B, N, H, D).transpose(0, 2, 1, 3)
    return mxq(a, 3, "e4m3") @ mxq(f, 2, "e4m3")

@@ -1,0 +1,259 @@
+from contextlib import ExitStack
+
+import concourse.mybir as mybir
+from concourse.masks import make_identity
+
+F32 = mybir.dt.float32
+BF16 = mybir.dt.bfloat16
+U32 = mybir.dt.uint32
+U8 = mybir.dt.uint8
+FP8X4 = mybir.dt.float8_e4m3fn_x4
+ALU = mybir.AluOpType
+ACT = mybir.ActivationFunctionType
+AXIS = mybir.AxisListType
+
+B, N, C, H, D, S = 4, 1024, 512, 4, 128, 128
+P = 128
+PACK = 4
+GROUP = P * PACK
+GROUPS_PER_BATCH = N // GROUP
+HALF = PACK // 2
+
+FLOPS = 2 * B * N * C * H * D + 2 * B * N * H * D * S + 2 * B * H * S * N * D
+
+
+def tile_physicsattentionbase_pa_kernel(tc, x, x_mid, Wfx, bfx, Wslice, bslice, temp, out):
+    nc = tc.nc
+    x_rows = x.rearrange("b n c -> (b n) c")
+    xm_rows = x_mid.rearrange("b n h d -> (b n) (h d)")
+
+    with ExitStack() as ctx:
+        consts = ctx.enter_context(tc.tile_pool(name="consts", bufs=1))
+        inputs = ctx.enter_context(tc.tile_pool(name="inputs", bufs=B * GROUPS_PER_BATCH))
+        work = ctx.enter_context(tc.tile_pool(name="work", bufs=2))
+        weights = ctx.enter_context(tc.tile_pool(name="weights", bufs=2 * GROUPS_PER_BATCH))
+        packed = ctx.enter_context(tc.tile_pool(name="packed", bufs=2 * GROUPS_PER_BATCH))
+        small = ctx.enter_context(tc.tile_pool(name="small", bufs=2 * GROUPS_PER_BATCH))
+        turn_ps = ctx.enter_context(tc.psum_pool(name="turn_ps", bufs=2))
+        z_pool = ctx.enter_context(tc.psum_pool(name="z_pool", bufs=2))
+        fx_pool = ctx.enter_context(tc.psum_pool(name="fx_pool", bufs=2))
+        batch_ps = ctx.enter_context(tc.psum_pool(name="batch_ps", bufs=2))
+
+        def load_group(rows, g, name):
+            tile_sb = inputs.tile([P, PACK * C], BF16, name=name)
+            nc.sync.dma_start(
+                out=tile_sb[:],
+                in_=rows[g * GROUP : (g + 1) * GROUP, :].rearrange("(p j) c -> p (j c)", j=PACK),
+            )
+            return tile_sb
+
+        wslice_sb = consts.tile([P, S], BF16)
+        nc.scalar.dma_start(out=wslice_sb[:], in_=Wslice)
+        bslice_col = consts.tile([P, 1], BF16)
+        nc.scalar.dma_start(out=bslice_col[:], in_=bslice.rearrange("(s o) -> s o", o=1))
+        temp_bc = consts.tile([P, H], BF16)
+        nc.scalar.dma_start(out=temp_bc[:], in_=temp.rearrange("a b h c -> (a b h c)").partition_broadcast(P))
+        bfx_bc = consts.tile([P, H * D], BF16)
+        nc.scalar.dma_start(out=bfx_bc[:], in_=bfx.partition_broadcast(P))
+
+        xm_tiles = []
+        x_tiles = []
+        xm_tiles.append(load_group(xm_rows, 0, "xm_sb"))
+        wfx_raw = consts.tile([P, PACK, H * D], BF16)
+        nc.sync.dma_start(
+            out=wfx_raw[:].rearrange("q (u e) n -> q u (e n)", u=2),
+            in_=Wfx.rearrange("(u q e) n -> q u (e n)", u=2, e=2),
+        )
+        x_tiles.append(load_group(x_rows, 0, "x_sb"))
+        for g in range(1, B * GROUPS_PER_BATCH):
+            xm_tiles.append(load_group(xm_rows, g, "xm_sb"))
+            x_tiles.append(load_group(x_rows, g, "x_sb"))
+
+        ident_f32 = consts.tile([P, P], F32)
+        make_identity(nc, ident_f32[:])
+        ident_bf16 = consts.tile([P, P], BF16)
+        make_identity(nc, ident_bf16[:])
+        bslice_rep = consts.tile([P, P], F32)
+        nc.vector.tensor_copy(out=bslice_rep[:], in_=bslice_col[:].to_broadcast([P, P]))
+        inv_temp = consts.tile([P, H], F32)
+        nc.vector.reciprocal(out=inv_temp[:], in_=temp_bc[:])
+        neg_inv_temp = consts.tile([P, H], F32)
+        nc.vector.tensor_scalar_mul(out=neg_inv_temp[:], in0=inv_temp[:], scalar1=-1.0)
+
+        wfx_grouped = consts.tile([P, H * D, PACK], BF16, align_bytes=64)
+        nc.vector.tensor_copy(out=wfx_grouped[:], in_=wfx_raw[:].rearrange("q t n -> q n t"))
+        wfx_codes = consts.tile([P, H * D], U32, align_bytes=64)
+        wfx_scales = consts.tile([P, H * D], U8, align_bytes=64)
+        nc.vector.quantize_mx(
+            out=wfx_codes[:].bitcast(FP8X4),
+            scales=wfx_scales[:],
+            in_=wfx_grouped[:].rearrange("q n t -> q (n t)"),
+        )
+
+        def softmax_weights(g):
+            xm_sb = xm_tiles[g]
+            xmT_sb = work.tile([P, PACK, H, P], BF16)
+            for half in range(2):
+                xmT_ps = turn_ps.tile([P, HALF, H, P], BF16, tag="turn")
+                for jl in range(HALF):
+                    for h in range(H):
+                        col = ((half * HALF + jl) * H + h) * D
+                        nc.tensor.transpose(xmT_ps[:, jl, h, :], xm_sb[:, col : col + D], ident_bf16[:])
+                nc.scalar.copy(out=xmT_sb[:, half * HALF : (half + 1) * HALF, :, :], in_=xmT_ps[:])
+
+            w_sb = weights.tile([P, PACK, H, S], F32)
+            row_max = small.tile([P, PACK, H], F32)
+            shift = small.tile([P, PACK, H], F32)
+            row_sum = small.tile([P, PACK, H], F32)
+            row_inv = small.tile([P, PACK, H], F32)
+            for j in range(PACK):
+                z_ps = z_pool.tile([P, H, S], F32)
+                for h in range(H):
+                    nc.tensor.matmul(
+                        z_ps[:, h, :], lhsT=xmT_sb[:, j, h, :], rhs=wslice_sb[:], start=True, stop=False
+                    )
+                    nc.tensor.matmul(
+                        z_ps[:, h, :],
+                        lhsT=bslice_rep[:],
+                        rhs=ident_f32[:],
+                        is_transpose=True,
+                        start=False,
+                        stop=True,
+                    )
+                nc.vector.tensor_reduce(out=row_max[:, j, :], in_=z_ps[:], axis=AXIS.X, op=ALU.max)
+                nc.vector.tensor_tensor(
+                    out=shift[:, j, :], in0=row_max[:, j, :], in1=neg_inv_temp[:], op=ALU.mult
+                )
+                for h in range(H):
+                    nc.scalar.activation(
+                        out=w_sb[:, j, h, :],
+                        in_=z_ps[:, h, :],
+                        func=ACT.Exp,
+                        bias=shift[:, j, h : h + 1],
+                        scale=inv_temp[:, h : h + 1],
+                        accum_out=row_sum[:, j, h : h + 1],
+                    )
+                nc.vector.reciprocal(out=row_inv[:, j, :], in_=row_sum[:, j, :])
+                for h in range(H):
+                    nc.scalar.activation(
+                        out=w_sb[:, j, h, :],
+                        in_=w_sb[:, j, h, :],
+                        func=ACT.Copy,
+                        scale=row_inv[:, j, h : h + 1],
+                    )
+            return w_sb
+
+        def quantised_fx(g):
+            x_words = x_tiles[g][:].bitcast(F32)
+            x_grouped = work.tile([P, PACK * P * PACK], BF16, align_bytes=64)
+            x_grouped_words = x_grouped[:].bitcast(F32).rearrange("q (j p u) -> q j p u", j=PACK, u=2)
+            for half in range(2):
+                xT_ps = turn_ps.tile([P, HALF, 2, P], F32, tag="turn")
+                for jl in range(HALF):
+                    for u in range(2):
+                        col = ((half * HALF + jl) * 2 + u) * P
+                        nc.tensor.transpose(xT_ps[:, jl, u, :], x_words[:, col : col + P], ident_f32[:])
+                nc.scalar.copy(
+                    out=x_grouped_words[:, half * HALF : (half + 1) * HALF, :, :],
+                    in_=xT_ps[:].rearrange("q jl u p -> q jl p u"),
+                )
+            x_codes = packed.tile([P, GROUP], U32, align_bytes=64)
+            x_scales = packed.tile([P, GROUP], U8, align_bytes=64)
+            nc.vector.quantize_mx(out=x_codes[:].bitcast(FP8X4), scales=x_scales[:], in_=x_grouped[:])
+
+            fx_grouped = work.tile([P, H, D, PACK], BF16, align_bytes=64)
+            for h in range(H):
+                fx_ps = fx_pool.tile([P, PACK, D], F32)
+                for j in range(PACK):
+                    nc.tensor.matmul_mx(
+                        out=fx_ps[:, j, :],
+                        lhsT=x_codes[:, j * P : (j + 1) * P].bitcast(FP8X4),
+                        lhsT_scale=x_scales[:, j * P : (j + 1) * P],
+                        rhs=wfx_codes[:, h * D : (h + 1) * D].bitcast(FP8X4),
+                        rhs_scale=wfx_scales[:, h * D : (h + 1) * D],
+                        start=True,
+                        stop=True,
+                    )
+                nc.vector.tensor_tensor(
+                    out=fx_grouped[:, h, :, :],
+                    in0=fx_ps[:].rearrange("p j d -> p d j"),
+                    in1=bfx_bc[:, h * D : (h + 1) * D].unsqueeze(2).to_broadcast([P, D, PACK]),
+                    op=ALU.add,
+                )
+            fx_codes = packed.tile([P, H * D], U32, align_bytes=64)
+            fx_scales = packed.tile([P, H * D], U8, align_bytes=64)
+            nc.vector.quantize_mx(
+                out=fx_codes[:].bitcast(FP8X4),
+                scales=fx_scales[:],
+                in_=fx_grouped[:].rearrange("p h d j -> p (h d j)"),
+            )
+            return fx_codes, fx_scales
+
+        def pool_batch(b, w_tiles, fx_operands):
+            wT_ps = batch_ps.tile([P, H, P], F32, tag="batch")
+            tiles_of_batch = [(w_sb, j) for w_sb in w_tiles for j in range(PACK)]
+            for h in range(H):
+                for i, (w_sb, j) in enumerate(tiles_of_batch):
+                    nc.tensor.matmul(
+                        wT_ps[:, h, :],
+                        lhsT=w_sb[:, j, h, :],
+                        rhs=ident_f32[:],
+                        is_transpose=True,
+                        start=(i == 0),
+                        stop=(i == len(tiles_of_batch) - 1),
+                    )
+            w_total = small.tile([P, H], F32)
+            nc.vector.tensor_reduce(out=w_total[:], in_=wT_ps[:], axis=AXIS.X, op=ALU.add)
+            mass = small.tile([P, H], F32)
+            nc.vector.tensor_scalar_add(out=mass[:], in0=w_total[:], scalar1=0.01)
+            inv_mass = small.tile([P, H], F32)
+            nc.vector.reciprocal(out=inv_mass[:], in_=mass[:])
+            inv_mass_ps = batch_ps.tile([P, H, S], F32, tag="batch")
+            for h in range(H):
+                nc.tensor.transpose(
+                    inv_mass_ps[:, h, :], inv_mass[:, h : h + 1].to_broadcast([P, P]), ident_f32[:]
+                )
+            inv_mass_bc = work.tile([P, H * S], F32)
+            nc.scalar.copy(out=inv_mass_bc[:], in_=inv_mass_ps[:].rearrange("p h s -> p (h s)"))
+
+            normed_operands = []
+            for w_sb in w_tiles:
+                normed_grouped = work.tile([P, H * S, PACK], BF16, align_bytes=64)
+                nc.vector.tensor_tensor(
+                    out=normed_grouped[:],
+                    in0=w_sb[:].rearrange("p j h s -> p (h s) j"),
+                    in1=inv_mass_bc[:].unsqueeze(2).to_broadcast([P, H * S, PACK]),
+                    op=ALU.mult,
+                )
+                normed_codes = packed.tile([P, H * S], U32, align_bytes=64)
+                normed_scales = packed.tile([P, H * S], U8, align_bytes=64)
+                nc.vector.quantize_mx(
+                    out=normed_codes[:].bitcast(FP8X4),
+                    scales=normed_scales[:],
+                    in_=normed_grouped[:].rearrange("p c j -> p (c j)"),
+                )
+                normed_operands.append((normed_codes, normed_scales))
+
+            out_ps = batch_ps.tile([P, H, D], F32, tag="batch")
+            for h in range(H):
+                for i in range(GROUPS_PER_BATCH):
+                    normed_codes, normed_scales = normed_operands[i]
+                    fx_codes, fx_scales = fx_operands[i]
+                    nc.tensor.matmul_mx(
+                        out=out_ps[:, h, :],
+                        lhsT=normed_codes[:, h * S : (h + 1) * S].bitcast(FP8X4),
+                        lhsT_scale=normed_scales[:, h * S : (h + 1) * S],
+                        rhs=fx_codes[:, h * D : (h + 1) * D].bitcast(FP8X4),
+                        rhs_scale=fx_scales[:, h * D : (h + 1) * D],
+                        start=(i == 0),
+                        stop=(i == GROUPS_PER_BATCH - 1),
+                    )
+            out_sb = work.tile([P, H, D], F32)
+            nc.scalar.copy(out=out_sb[:], in_=out_ps[:])
+            nc.sync.dma_start(out=out[b].rearrange("h s d -> s h d"), in_=out_sb[:])
+
+        for b in range(B):
+            groups = [b * GROUPS_PER_BATCH + i for i in range(GROUPS_PER_BATCH)]
+            w_tiles = [softmax_weights(g) for g in groups]
+            fx_operands = [quantised_fx(g) for g in groups]
+            pool_batch(b, w_tiles, fx_operands)

@@ -17,7 +17,10 @@ P = 128
 PACK = 4
 GROUP = P * PACK
 GROUPS_PER_BATCH = N // GROUP
-HALF = PACK // 2
+UNITS_PER_BATCH = H * GROUPS_PER_BATCH
+UNITS = B * UNITS_PER_BATCH
+XUNITS_PER_BATCH = GROUPS_PER_BATCH * PACK
+MASS_N = 128
 
 FLOPS = 2 * B * N * C * H * D + 2 * B * N * H * D * S + 2 * B * H * S * N * D
 
@@ -30,14 +33,15 @@ def tile_physicsattentionbase_pa_kernel(tc, x, x_mid, Wfx, bfx, Wslice, bslice, 
     with ExitStack() as ctx:
         consts = ctx.enter_context(tc.tile_pool(name="consts", bufs=1))
         inputs = ctx.enter_context(tc.tile_pool(name="inputs", bufs=B * GROUPS_PER_BATCH))
-        work = ctx.enter_context(tc.tile_pool(name="work", bufs=2))
-        weights = ctx.enter_context(tc.tile_pool(name="weights", bufs=2 * GROUPS_PER_BATCH))
-        packed = ctx.enter_context(tc.tile_pool(name="packed", bufs=2 * GROUPS_PER_BATCH))
-        small = ctx.enter_context(tc.tile_pool(name="small", bufs=2 * GROUPS_PER_BATCH))
-        turn_ps = ctx.enter_context(tc.psum_pool(name="turn_ps", bufs=2))
+        work = ctx.enter_context(tc.tile_pool(name="work", bufs=3))
+        wide = ctx.enter_context(tc.tile_pool(name="wide", bufs=7))
+        packed = ctx.enter_context(tc.tile_pool(name="packed", bufs=6))
+        xpacked = ctx.enter_context(tc.tile_pool(name="xpacked", bufs=2 * XUNITS_PER_BATCH + 4))
+        small = ctx.enter_context(tc.tile_pool(name="small", bufs=6))
         z_pool = ctx.enter_context(tc.psum_pool(name="z_pool", bufs=2))
-        fx_pool = ctx.enter_context(tc.psum_pool(name="fx_pool", bufs=2))
-        batch_ps = ctx.enter_context(tc.psum_pool(name="batch_ps", bufs=2))
+        one_ps = ctx.enter_context(tc.psum_pool(name="one_ps", bufs=1))
+
+        ctx.enter_context(tc.manual_schedule())
 
         def load_group(rows, g, name):
             tile_sb = inputs.tile([P, PACK * C], BF16, name=name)
@@ -53,26 +57,34 @@ def tile_physicsattentionbase_pa_kernel(tc, x, x_mid, Wfx, bfx, Wslice, bslice, 
         nc.scalar.dma_start(out=bslice_col[:], in_=bslice.rearrange("(s o) -> s o", o=1))
         temp_bc = consts.tile([P, H], BF16)
         nc.scalar.dma_start(out=temp_bc[:], in_=temp.rearrange("a b h c -> (a b h c)").partition_broadcast(P))
-        bfx_bc = consts.tile([P, H * D], BF16)
-        nc.scalar.dma_start(out=bfx_bc[:], in_=bfx.partition_broadcast(P))
 
-        xm_tiles = []
-        x_tiles = []
-        xm_tiles.append(load_group(xm_rows, 0, "xm_sb"))
+        xm_tiles = {}
+        x_tiles = {}
+        xm_tiles[0] = load_group(xm_rows, 0, "xm_sb")
+        xm_tiles[1] = load_group(xm_rows, 1, "xm_sb")
+        x_tiles[0] = load_group(x_rows, 0, "x_sb")
         wfx_raw = consts.tile([P, PACK, H * D], BF16)
         nc.sync.dma_start(
             out=wfx_raw[:].rearrange("q (u e) n -> q u (e n)", u=2),
             in_=Wfx.rearrange("(u q e) n -> q u (e n)", u=2, e=2),
         )
-        x_tiles.append(load_group(x_rows, 0, "x_sb"))
-        for g in range(1, B * GROUPS_PER_BATCH):
-            xm_tiles.append(load_group(xm_rows, g, "xm_sb"))
-            x_tiles.append(load_group(x_rows, g, "x_sb"))
+        x_tiles[1] = load_group(x_rows, 1, "x_sb")
+        bfx_bc = consts.tile([P, H * D], BF16)
+        nc.sync.dma_start(out=bfx_bc[:], in_=bfx.partition_broadcast(P))
+        for g in range(2, B * GROUPS_PER_BATCH):
+            xm_tiles[g] = load_group(xm_rows, g, "xm_sb")
+            x_tiles[g] = load_group(x_rows, g, "x_sb")
 
-        ident_f32 = consts.tile([P, P], F32)
-        make_identity(nc, ident_f32[:])
         ident_bf16 = consts.tile([P, P], BF16)
         make_identity(nc, ident_bf16[:])
+        ident_f32 = consts.tile([P, P], F32)
+        make_identity(nc, ident_f32[:])
+        ones_f32 = consts.tile([P, MASS_N], F32)
+        nc.gpsimd.memset(ones_f32[:], 1.0)
+        zero_col = consts.tile([P, 1], F32)
+        nc.vector.memset(zero_col[:], 0.0)
+        warm_col = consts.tile([P, 1], F32)
+        nc.scalar.activation(out=warm_col[:], in_=zero_col[:], func=ACT.Exp)
         bslice_rep = consts.tile([P, P], F32)
         nc.vector.tensor_copy(out=bslice_rep[:], in_=bslice_col[:].to_broadcast([P, P]))
         inv_temp = consts.tile([P, H], F32)
@@ -80,180 +92,291 @@ def tile_physicsattentionbase_pa_kernel(tc, x, x_mid, Wfx, bfx, Wslice, bslice, 
         neg_inv_temp = consts.tile([P, H], F32)
         nc.vector.tensor_scalar_mul(out=neg_inv_temp[:], in0=inv_temp[:], scalar1=-1.0)
 
-        wfx_grouped = consts.tile([P, H * D, PACK], BF16, align_bytes=64)
-        nc.vector.tensor_copy(out=wfx_grouped[:], in_=wfx_raw[:].rearrange("q t n -> q n t"))
-        wfx_codes = consts.tile([P, H * D], U32, align_bytes=64)
-        wfx_scales = consts.tile([P, H * D], U8, align_bytes=64)
-        nc.vector.quantize_mx(
-            out=wfx_codes[:].bitcast(FP8X4),
-            scales=wfx_scales[:],
-            in_=wfx_grouped[:].rearrange("q n t -> q (n t)"),
-        )
+        wfx_ops = {}
 
-        def softmax_weights(g):
-            xm_sb = xm_tiles[g]
-            xmT_sb = work.tile([P, PACK, H, P], BF16)
-            for half in range(2):
-                xmT_ps = turn_ps.tile([P, HALF, H, P], BF16, tag="turn")
-                for jl in range(HALF):
-                    for h in range(H):
-                        col = ((half * HALF + jl) * H + h) * D
-                        nc.tensor.transpose(xmT_ps[:, jl, h, :], xm_sb[:, col : col + D], ident_bf16[:])
-                nc.scalar.copy(out=xmT_sb[:, half * HALF : (half + 1) * HALF, :, :], in_=xmT_ps[:])
-
-            w_sb = weights.tile([P, PACK, H, S], F32)
-            row_max = small.tile([P, PACK, H], F32)
-            shift = small.tile([P, PACK, H], F32)
-            row_sum = small.tile([P, PACK, H], F32)
-            row_inv = small.tile([P, PACK, H], F32)
-            for j in range(PACK):
-                z_ps = z_pool.tile([P, H, S], F32)
-                for h in range(H):
-                    nc.tensor.matmul(
-                        z_ps[:, h, :], lhsT=xmT_sb[:, j, h, :], rhs=wslice_sb[:], start=True, stop=False
-                    )
-                    nc.tensor.matmul(
-                        z_ps[:, h, :],
-                        lhsT=bslice_rep[:],
-                        rhs=ident_f32[:],
-                        is_transpose=True,
-                        start=False,
-                        stop=True,
-                    )
-                nc.vector.tensor_reduce(out=row_max[:, j, :], in_=z_ps[:], axis=AXIS.X, op=ALU.max)
-                nc.vector.tensor_tensor(
-                    out=shift[:, j, :], in0=row_max[:, j, :], in1=neg_inv_temp[:], op=ALU.mult
-                )
-                for h in range(H):
-                    nc.scalar.activation(
-                        out=w_sb[:, j, h, :],
-                        in_=z_ps[:, h, :],
-                        func=ACT.Exp,
-                        bias=shift[:, j, h : h + 1],
-                        scale=inv_temp[:, h : h + 1],
-                        accum_out=row_sum[:, j, h : h + 1],
-                    )
-                nc.vector.reciprocal(out=row_inv[:, j, :], in_=row_sum[:, j, :])
-                for h in range(H):
-                    nc.scalar.activation(
-                        out=w_sb[:, j, h, :],
-                        in_=w_sb[:, j, h, :],
-                        func=ACT.Copy,
-                        scale=row_inv[:, j, h : h + 1],
-                    )
-            return w_sb
-
-        def quantised_fx(g):
-            x_words = x_tiles[g][:].bitcast(F32)
-            x_grouped = work.tile([P, PACK * P * PACK], BF16, align_bytes=64)
-            x_grouped_words = x_grouped[:].bitcast(F32).rearrange("q (j p u) -> q j p u", j=PACK, u=2)
-            for half in range(2):
-                xT_ps = turn_ps.tile([P, HALF, 2, P], F32, tag="turn")
-                for jl in range(HALF):
-                    for u in range(2):
-                        col = ((half * HALF + jl) * 2 + u) * P
-                        nc.tensor.transpose(xT_ps[:, jl, u, :], x_words[:, col : col + P], ident_f32[:])
-                nc.scalar.copy(
-                    out=x_grouped_words[:, half * HALF : (half + 1) * HALF, :, :],
-                    in_=xT_ps[:].rearrange("q jl u p -> q jl p u"),
-                )
-            x_codes = packed.tile([P, GROUP], U32, align_bytes=64)
-            x_scales = packed.tile([P, GROUP], U8, align_bytes=64)
-            nc.vector.quantize_mx(out=x_codes[:].bitcast(FP8X4), scales=x_scales[:], in_=x_grouped[:])
-
-            fx_grouped = work.tile([P, H, D, PACK], BF16, align_bytes=64)
-            for h in range(H):
-                fx_ps = fx_pool.tile([P, PACK, D], F32)
-                for j in range(PACK):
-                    nc.tensor.matmul_mx(
-                        out=fx_ps[:, j, :],
-                        lhsT=x_codes[:, j * P : (j + 1) * P].bitcast(FP8X4),
-                        lhsT_scale=x_scales[:, j * P : (j + 1) * P],
-                        rhs=wfx_codes[:, h * D : (h + 1) * D].bitcast(FP8X4),
-                        rhs_scale=wfx_scales[:, h * D : (h + 1) * D],
-                        start=True,
-                        stop=True,
-                    )
-                nc.vector.tensor_tensor(
-                    out=fx_grouped[:, h, :, :],
-                    in0=fx_ps[:].rearrange("p j d -> p d j"),
-                    in1=bfx_bc[:, h * D : (h + 1) * D].unsqueeze(2).to_broadcast([P, D, PACK]),
-                    op=ALU.add,
-                )
-            fx_codes = packed.tile([P, H * D], U32, align_bytes=64)
-            fx_scales = packed.tile([P, H * D], U8, align_bytes=64)
-            nc.vector.quantize_mx(
-                out=fx_codes[:].bitcast(FP8X4),
-                scales=fx_scales[:],
-                in_=fx_grouped[:].rearrange("p h d j -> p (h d j)"),
+        def wfx_copy(h):
+            grouped = consts.tile([P, D, PACK], BF16, align_bytes=64, name="wfx_grouped%d" % h)
+            nc.vector.tensor_copy(
+                out=grouped[:], in_=wfx_raw[:, :, h * D : (h + 1) * D].rearrange("q t n -> q n t")
             )
-            return fx_codes, fx_scales
+            wfx_ops[h] = grouped
 
-        def pool_batch(b, w_tiles, fx_operands):
-            wT_ps = batch_ps.tile([P, H, P], F32, tag="batch")
-            tiles_of_batch = [(w_sb, j) for w_sb in w_tiles for j in range(PACK)]
-            for h in range(H):
-                for i, (w_sb, j) in enumerate(tiles_of_batch):
-                    nc.tensor.matmul(
-                        wT_ps[:, h, :],
-                        lhsT=w_sb[:, j, h, :],
-                        rhs=ident_f32[:],
-                        is_transpose=True,
-                        start=(i == 0),
-                        stop=(i == len(tiles_of_batch) - 1),
-                    )
-            w_total = small.tile([P, H], F32)
-            nc.vector.tensor_reduce(out=w_total[:], in_=wT_ps[:], axis=AXIS.X, op=ALU.add)
-            mass = small.tile([P, H], F32)
-            nc.vector.tensor_scalar_add(out=mass[:], in0=w_total[:], scalar1=0.01)
-            inv_mass = small.tile([P, H], F32)
-            nc.vector.reciprocal(out=inv_mass[:], in_=mass[:])
-            inv_mass_ps = batch_ps.tile([P, H, S], F32, tag="batch")
-            for h in range(H):
-                nc.tensor.transpose(
-                    inv_mass_ps[:, h, :], inv_mass[:, h : h + 1].to_broadcast([P, P]), ident_f32[:]
+        def wfx_quantise(h):
+            grouped = wfx_ops[h]
+            codes = consts.tile([P, D], U32, align_bytes=64, name="wfx_codes%d" % h)
+            scales = consts.tile([P, D], U8, align_bytes=64, name="wfx_scales%d" % h)
+            nc.vector.quantize_mx(
+                out=codes[:].bitcast(FP8X4), scales=scales[:], in_=grouped[:].rearrange("q n t -> q (n t)")
+            )
+            wfx_ops[h] = (codes, scales)
+
+        def place(u):
+            b, r = divmod(u, UNITS_PER_BATCH)
+            h, i = divmod(r, GROUPS_PER_BATCH)
+            return b, h, i, b * GROUPS_PER_BATCH + i
+
+        st = {}
+
+        def xm_turn(u):
+            b, h, i, g = place(u)
+            ps = one_ps.tile([P, PACK, P], BF16, name="xmT_ps")
+            for j in range(PACK):
+                col = (j * H + h) * D
+                nc.tensor.transpose(ps[:, j, :], xm_tiles[g][:, col : col + D], ident_bf16[:])
+            st["xmT_ps", u] = ps
+
+        def xm_copy(u):
+            sb = work.tile([P, PACK, P], BF16, name="xmT_sb")
+            nc.scalar.copy(out=sb[:], in_=st["xmT_ps", u][:])
+            st["xmT", u] = sb
+
+        def x_turn(vs):
+            ps = one_ps.tile([P, 2, 2, P], F32, name="xT_ps")
+            for n, v in enumerate(vs):
+                g, j = divmod(v, PACK)
+                words = x_tiles[g][:].bitcast(F32)
+                for e in range(2):
+                    col = (j * 2 + e) * P
+                    nc.tensor.transpose(ps[:, n, e, :], words[:, col : col + P], ident_f32[:])
+            st["xT_ps", vs[0]] = ps
+
+        def x_copy(vs):
+            ps = st["xT_ps", vs[0]]
+            for n, v in enumerate(vs):
+                grouped = work.tile([P, P * PACK], BF16, align_bytes=64, name="x_grouped")
+                nc.scalar.copy(
+                    out=grouped[:].bitcast(F32).rearrange("q (p u) -> q p u", u=2),
+                    in_=ps[:, n, :, :].rearrange("q u p -> q p u"),
                 )
-            inv_mass_bc = work.tile([P, H * S], F32)
-            nc.scalar.copy(out=inv_mass_bc[:], in_=inv_mass_ps[:].rearrange("p h s -> p (h s)"))
+                st["x_grouped", v] = grouped
 
-            normed_operands = []
-            for w_sb in w_tiles:
-                normed_grouped = work.tile([P, H * S, PACK], BF16, align_bytes=64)
-                nc.vector.tensor_tensor(
-                    out=normed_grouped[:],
-                    in0=w_sb[:].rearrange("p j h s -> p (h s) j"),
-                    in1=inv_mass_bc[:].unsqueeze(2).to_broadcast([P, H * S, PACK]),
-                    op=ALU.mult,
+        def x_quantise(v):
+            codes = xpacked.tile([P, P], U32, align_bytes=64, name="x_codes")
+            scales = xpacked.tile([P, P], U8, align_bytes=64, name="x_scales")
+            nc.vector.quantize_mx(
+                out=codes[:].bitcast(FP8X4), scales=scales[:], in_=st["x_grouped", v][:]
+            )
+            st["x_ops", v] = (codes, scales)
+
+        def logits(u):
+            xmT = st["xmT", u]
+            ps = z_pool.tile([P, PACK, S], F32, name="z_ps")
+            for j in range(PACK):
+                nc.tensor.matmul(
+                    ps[:, j, :], lhsT=bslice_rep[:], rhs=ident_f32[:], is_transpose=True, start=(j == 0), stop=False
                 )
-                normed_codes = packed.tile([P, H * S], U32, align_bytes=64)
-                normed_scales = packed.tile([P, H * S], U8, align_bytes=64)
-                nc.vector.quantize_mx(
-                    out=normed_codes[:].bitcast(FP8X4),
-                    scales=normed_scales[:],
-                    in_=normed_grouped[:].rearrange("p c j -> p (c j)"),
+            for j in range(PACK):
+                nc.tensor.matmul(
+                    ps[:, j, :], lhsT=xmT[:, j, :], rhs=wslice_sb[:], start=False, stop=(j == PACK - 1)
                 )
-                normed_operands.append((normed_codes, normed_scales))
+            st["z", u] = ps
 
-            out_ps = batch_ps.tile([P, H, D], F32, tag="batch")
-            for h in range(H):
-                for i in range(GROUPS_PER_BATCH):
-                    normed_codes, normed_scales = normed_operands[i]
-                    fx_codes, fx_scales = fx_operands[i]
-                    nc.tensor.matmul_mx(
-                        out=out_ps[:, h, :],
-                        lhsT=normed_codes[:, h * S : (h + 1) * S].bitcast(FP8X4),
-                        lhsT_scale=normed_scales[:, h * S : (h + 1) * S],
-                        rhs=fx_codes[:, h * D : (h + 1) * D].bitcast(FP8X4),
-                        rhs_scale=fx_scales[:, h * D : (h + 1) * D],
-                        start=(i == 0),
-                        stop=(i == GROUPS_PER_BATCH - 1),
-                    )
-            out_sb = work.tile([P, H, D], F32)
-            nc.scalar.copy(out=out_sb[:], in_=out_ps[:])
-            nc.sync.dma_start(out=out[b].rearrange("h s d -> s h d"), in_=out_sb[:])
+        def row_max(u):
+            m = small.tile([P, PACK], F32, name="row_max")
+            nc.vector.tensor_reduce(out=m[:], in_=st["z", u][:], axis=AXIS.X, op=ALU.max)
+            st["max", u] = m
 
-        for b in range(B):
-            groups = [b * GROUPS_PER_BATCH + i for i in range(GROUPS_PER_BATCH)]
-            w_tiles = [softmax_weights(g) for g in groups]
-            fx_operands = [quantised_fx(g) for g in groups]
-            pool_batch(b, w_tiles, fx_operands)
+        def row_shift(u):
+            b, h, i, g = place(u)
+            shift = small.tile([P, PACK], F32, name="shift")
+            nc.scalar.activation(
+                out=shift[:], in_=st["max", u][:], func=ACT.Copy, scale=neg_inv_temp[:, h : h + 1]
+            )
+            st["shift", u] = shift
+
+        def exps(u):
+            b, h, i, g = place(u)
+            ps, shift = st["z", u], st["shift", u]
+            w = wide.tile([P, PACK, S], F32, name="w_sb")
+            row_sum = small.tile([P, PACK], F32, name="row_sum")
+            for j in range(PACK):
+                nc.scalar.activation(
+                    out=w[:, j, :],
+                    in_=ps[:, j, :],
+                    func=ACT.Exp,
+                    bias=shift[:, j : j + 1],
+                    scale=inv_temp[:, h : h + 1],
+                    accum_out=row_sum[:, j : j + 1],
+                )
+            st["w", u] = w
+            st["sum", u] = row_sum
+
+        def row_inverse(u):
+            r = small.tile([P, PACK], F32, name="row_inv")
+            nc.vector.reciprocal(out=r[:], in_=st["sum", u][:])
+            st["inv", u] = r
+
+        def scale_rows(u):
+            w, r = st["w", u], st["inv", u]
+            for j in range(PACK):
+                nc.scalar.activation(out=w[:, j, :], in_=w[:, j, :], func=ACT.Copy, scale=r[:, j : j + 1])
+
+        def point_sum(u):
+            w = st["w", u]
+            pair = small.tile([P, 2, S], F32, name="pair")
+            nc.gpsimd.tensor_tensor(out=pair[:], in0=w[:, 0:2, :], in1=w[:, 2:4, :], op=ALU.add)
+            tot = small.tile([P, S], F32, name="tot")
+            nc.gpsimd.tensor_tensor(out=tot[:], in0=pair[:, 0, :], in1=pair[:, 1, :], op=ALU.add)
+            st["tot", u] = tot
+
+        def mass_sum(u):
+            b, h, i, g = place(u)
+            if i == 0:
+                st["mass", u // 2] = one_ps.tile([P, MASS_N], F32, name="mass_ps")
+            nc.tensor.matmul(
+                st["mass", u // 2][:],
+                lhsT=st["tot", u][:],
+                rhs=ones_f32[:],
+                start=(i == 0),
+                stop=(i == GROUPS_PER_BATCH - 1),
+            )
+
+        def mass_add(k):
+            m = small.tile([P, 1], F32, name="mass")
+            nc.scalar.activation(out=m[:], in_=st["mass", k][:, 0:1], func=ACT.Copy, bias=0.01)
+            st["mass1", k] = m
+
+        def mass_inverse(k):
+            r = small.tile([P, 1], F32, name="inv_mass")
+            nc.vector.reciprocal(out=r[:], in_=st["mass1", k][:])
+            st["minv", k] = r
+
+        def spread(k):
+            ps = one_ps.tile([P, S], F32, name="inv_mass_ps")
+            nc.tensor.transpose(ps[:], st["minv", k][:].to_broadcast([P, P]), ident_f32[:])
+            st["spread", k] = ps
+
+        def normed(u):
+            b, h, i, g = place(u)
+            grouped = work.tile([P, S, PACK], BF16, align_bytes=64, name="normed_grouped")
+            nc.vector.tensor_tensor(
+                out=grouped[:],
+                in0=st["w", u][:].rearrange("p j s -> p s j"),
+                in1=st["spread", u // 2][:].unsqueeze(2).to_broadcast([P, S, PACK]),
+                op=ALU.mult,
+            )
+            st["normed", u] = grouped
+
+        def quantise(kind, u):
+            grouped = st[kind, u]
+            codes = packed.tile([P, P], U32, align_bytes=64, name=kind + "_codes")
+            scales = packed.tile([P, P], U8, align_bytes=64, name=kind + "_scales")
+            nc.vector.quantize_mx(
+                out=codes[:].bitcast(FP8X4), scales=scales[:], in_=grouped[:].rearrange("p s j -> p (s j)")
+            )
+            st[kind + "_ops", u] = (codes, scales)
+
+        def fx_matmul(u):
+            b, h, i, g = place(u)
+            ps = one_ps.tile([P, PACK, D], F32, name="fx_ps")
+            w_codes, w_scales = wfx_ops[h]
+            for j in range(PACK):
+                x_codes, x_scales = st["x_ops", g * PACK + j]
+                nc.tensor.matmul_mx(
+                    out=ps[:, j, :],
+                    lhsT=x_codes[:].bitcast(FP8X4),
+                    lhsT_scale=x_scales[:],
+                    rhs=w_codes[:].bitcast(FP8X4),
+                    rhs_scale=w_scales[:],
+                    start=True,
+                    stop=True,
+                )
+            st["fx_ps", u] = ps
+
+        def fx_bias(u):
+            b, h, i, g = place(u)
+            grouped = work.tile([P, D, PACK], BF16, align_bytes=64, name="fx_grouped")
+            nc.vector.tensor_tensor(
+                out=grouped[:],
+                in0=st["fx_ps", u][:].rearrange("p j d -> p d j"),
+                in1=bfx_bc[:, h * D : (h + 1) * D].unsqueeze(2).to_broadcast([P, D, PACK]),
+                op=ALU.add,
+            )
+            st["fx", u] = grouped
+
+        def pool_matmul(k):
+            ps = one_ps.tile([P, D], F32, name="out_ps")
+            for i in range(GROUPS_PER_BATCH):
+                n_codes, n_scales = st["normed_ops", 2 * k + i]
+                f_codes, f_scales = st["fx_ops", 2 * k + i]
+                nc.tensor.matmul_mx(
+                    out=ps[:],
+                    lhsT=n_codes[:].bitcast(FP8X4),
+                    lhsT_scale=n_scales[:],
+                    rhs=f_codes[:].bitcast(FP8X4),
+                    rhs_scale=f_scales[:],
+                    start=(i == 0),
+                    stop=(i == GROUPS_PER_BATCH - 1),
+                )
+            st["out_ps", k] = ps
+
+        def store(k):
+            b, h = divmod(k, H)
+            sb = work.tile([P, D], F32, name="out_sb")
+            nc.scalar.copy(out=sb[:], in_=st["out_ps", k][:])
+            nc.sync.dma_start(out=out[b, h], in_=sb[:])
+
+        x_plan = {}
+        v, t = 0, 1
+        while v < B * XUNITS_PER_BATCH:
+            n = 2 if v < XUNITS_PER_BATCH else 1
+            x_plan[t] = list(range(v, min(v + n, B * XUNITS_PER_BATCH)))
+            v += n
+            t += 1
+
+        def has(u):
+            return 0 <= u < UNITS
+
+        def ends_head(u):
+            return has(u) and u % GROUPS_PER_BATCH == GROUPS_PER_BATCH - 1
+
+        for t in range(-2, UNITS + 9):
+            xs = x_plan.get(t, [])
+            xq = x_plan.get(t - 1, [])
+            if has(t):
+                logits(t)
+            if has(t - 3):
+                mass_sum(t - 3)
+            if has(t - 5):
+                fx_matmul(t - 5)
+            if ends_head(t - 6):
+                pool_matmul((t - 6) // 2)
+            if ends_head(t - 4):
+                spread((t - 4) // 2)
+            if has(t + 2):
+                xm_turn(t + 2)
+            if xs:
+                x_turn(xs)
+            if has(t):
+                row_max(t)
+            if has(t - 1):
+                row_inverse(t - 1)
+            if ends_head(t - 7):
+                store((t - 7) // 2)
+            if ends_head(t - 3):
+                mass_add((t - 3) // 2)
+            if has(t):
+                row_shift(t)
+                exps(t)
+            if has(t + 2):
+                xm_copy(t + 2)
+            if xs:
+                x_copy(xs)
+            if has(t - 1):
+                scale_rows(t - 1)
+                point_sum(t - 1)
+            if 0 <= t < H:
+                wfx_copy(t)
+            for v in xq:
+                x_quantise(v)
+            if has(t - 5):
+                fx_bias(t - 5)
+            if 0 <= t < H:
+                wfx_quantise(t)
+            if has(t - 5):
+                normed(t - 5)
+                quantise("fx", t - 5)
+            if ends_head(t - 3):
+                mass_inverse((t - 3) // 2)
+            if has(t - 5):
+                quantise("normed", t - 5)

@@ -61,13 +61,13 @@ def tile_physicsattentionbase_pa_kernel(tc, x, x_mid, Wfx, bfx, Wslice, bslice, 
         xm_tiles = {}
         x_tiles = {}
         xm_tiles[0] = load_group(xm_rows, 0, "xm_sb")
-        xm_tiles[1] = load_group(xm_rows, 1, "xm_sb")
-        x_tiles[0] = load_group(x_rows, 0, "x_sb")
         wfx_raw = consts.tile([P, PACK, H * D], BF16)
         nc.sync.dma_start(
             out=wfx_raw[:].rearrange("q (u e) n -> q u (e n)", u=2),
             in_=Wfx.rearrange("(u q e) n -> q u (e n)", u=2, e=2),
         )
+        x_tiles[0] = load_group(x_rows, 0, "x_sb")
+        xm_tiles[1] = load_group(xm_rows, 1, "xm_sb")
         x_tiles[1] = load_group(x_rows, 1, "x_sb")
         bfx_bc = consts.tile([P, H * D], BF16)
         nc.sync.dma_start(out=bfx_bc[:], in_=bfx.partition_broadcast(P))
@@ -92,23 +92,23 @@ def tile_physicsattentionbase_pa_kernel(tc, x, x_mid, Wfx, bfx, Wslice, bslice, 
         neg_inv_temp = consts.tile([P, H], F32)
         nc.vector.tensor_scalar_mul(out=neg_inv_temp[:], in0=inv_temp[:], scalar1=-1.0)
 
-        wfx_ops = {}
+        wfx_grouped = consts.tile([P, H * D, PACK], BF16, align_bytes=64)
+        wfx_codes = consts.tile([P, H * D], U32, align_bytes=64)
+        wfx_scales = consts.tile([P, H * D], U8, align_bytes=64)
 
         def wfx_copy(h):
-            grouped = consts.tile([P, D, PACK], BF16, align_bytes=64, name="wfx_grouped%d" % h)
-            nc.vector.tensor_copy(
-                out=grouped[:], in_=wfx_raw[:, :, h * D : (h + 1) * D].rearrange("q t n -> q n t")
-            )
-            wfx_ops[h] = grouped
+            cols = slice(h * D, (h + 1) * D)
+            nc.vector.tensor_copy(out=wfx_grouped[:, cols, :], in_=wfx_raw[:, :, cols].rearrange("q t n -> q n t"))
+            st["wc", h] = 1
 
         def wfx_quantise(h):
-            grouped = wfx_ops[h]
-            codes = consts.tile([P, D], U32, align_bytes=64, name="wfx_codes%d" % h)
-            scales = consts.tile([P, D], U8, align_bytes=64, name="wfx_scales%d" % h)
+            st["wq", h] = st["wc", h]
+            cols = slice(h * D, (h + 1) * D)
             nc.vector.quantize_mx(
-                out=codes[:].bitcast(FP8X4), scales=scales[:], in_=grouped[:].rearrange("q n t -> q (n t)")
+                out=wfx_codes[:, cols].bitcast(FP8X4),
+                scales=wfx_scales[:, cols],
+                in_=wfx_grouped[:, cols, :].rearrange("q n t -> q (n t)"),
             )
-            wfx_ops[h] = (codes, scales)
 
         def place(u):
             b, r = divmod(u, UNITS_PER_BATCH)
@@ -210,9 +210,10 @@ def tile_physicsattentionbase_pa_kernel(tc, x, x_mid, Wfx, bfx, Wslice, bslice, 
             w, r = st["w", u], st["inv", u]
             for j in range(PACK):
                 nc.scalar.activation(out=w[:, j, :], in_=w[:, j, :], func=ACT.Copy, scale=r[:, j : j + 1])
+            st["ws", u] = w
 
         def point_sum(u):
-            w = st["w", u]
+            w = st["ws", u]
             pair = small.tile([P, 2, S], F32, name="pair")
             nc.gpsimd.tensor_tensor(out=pair[:], in0=w[:, 0:2, :], in1=w[:, 2:4, :], op=ALU.add)
             tot = small.tile([P, S], F32, name="tot")
@@ -230,10 +231,12 @@ def tile_physicsattentionbase_pa_kernel(tc, x, x_mid, Wfx, bfx, Wslice, bslice, 
                 start=(i == 0),
                 stop=(i == GROUPS_PER_BATCH - 1),
             )
+            if i == GROUPS_PER_BATCH - 1:
+                st["mass_done", u // 2] = st["mass", u // 2]
 
         def mass_add(k):
             m = small.tile([P, 1], F32, name="mass")
-            nc.scalar.activation(out=m[:], in_=st["mass", k][:, 0:1], func=ACT.Copy, bias=0.01)
+            nc.scalar.activation(out=m[:], in_=st["mass_done", k][:, 0:1], func=ACT.Copy, bias=0.01)
             st["mass1", k] = m
 
         def mass_inverse(k):
@@ -251,7 +254,7 @@ def tile_physicsattentionbase_pa_kernel(tc, x, x_mid, Wfx, bfx, Wslice, bslice, 
             grouped = work.tile([P, S, PACK], BF16, align_bytes=64, name="normed_grouped")
             nc.vector.tensor_tensor(
                 out=grouped[:],
-                in0=st["w", u][:].rearrange("p j s -> p s j"),
+                in0=st["ws", u][:].rearrange("p j s -> p s j"),
                 in1=st["spread", u // 2][:].unsqueeze(2).to_broadcast([P, S, PACK]),
                 op=ALU.mult,
             )
@@ -268,16 +271,17 @@ def tile_physicsattentionbase_pa_kernel(tc, x, x_mid, Wfx, bfx, Wslice, bslice, 
 
         def fx_matmul(u):
             b, h, i, g = place(u)
+            assert st["wq", h]
             ps = one_ps.tile([P, PACK, D], F32, name="fx_ps")
-            w_codes, w_scales = wfx_ops[h]
+            cols = slice(h * D, (h + 1) * D)
             for j in range(PACK):
                 x_codes, x_scales = st["x_ops", g * PACK + j]
                 nc.tensor.matmul_mx(
                     out=ps[:, j, :],
                     lhsT=x_codes[:].bitcast(FP8X4),
                     lhsT_scale=x_scales[:],
-                    rhs=w_codes[:].bitcast(FP8X4),
-                    rhs_scale=w_scales[:],
+                    rhs=wfx_codes[:, cols].bitcast(FP8X4),
+                    rhs_scale=wfx_scales[:, cols],
                     start=True,
                     stop=True,
                 )
@@ -317,9 +321,9 @@ def tile_physicsattentionbase_pa_kernel(tc, x, x_mid, Wfx, bfx, Wslice, bslice, 
             nc.sync.dma_start(out=out[b, h], in_=sb[:])
 
         x_plan = {}
-        v, t = 0, 1
+        v, t = 0, -1
         while v < B * XUNITS_PER_BATCH:
-            n = 2 if v < XUNITS_PER_BATCH else 1
+            n = 2 if v < 8 else 1
             x_plan[t] = list(range(v, min(v + n, B * XUNITS_PER_BATCH)))
             v += n
             t += 1
@@ -330,53 +334,55 @@ def tile_physicsattentionbase_pa_kernel(tc, x, x_mid, Wfx, bfx, Wslice, bslice, 
         def ends_head(u):
             return has(u) and u % GROUPS_PER_BATCH == GROUPS_PER_BATCH - 1
 
-        for t in range(-2, UNITS + 9):
+        for t in range(-4, UNITS + 12):
             xs = x_plan.get(t, [])
-            xq = x_plan.get(t - 1, [])
+            if 0 <= t + 2 < H:
+                wfx_copy(t + 2)
+            if 0 <= t + 2 < H:
+                wfx_quantise(t + 2)
             if has(t):
                 logits(t)
+            for v in x_plan.get(t - 1, []):
+                x_quantise(v)
             if has(t - 3):
-                mass_sum(t - 3)
-            if has(t - 5):
-                fx_matmul(t - 5)
-            if ends_head(t - 6):
-                pool_matmul((t - 6) // 2)
-            if ends_head(t - 4):
-                spread((t - 4) // 2)
-            if has(t + 2):
-                xm_turn(t + 2)
+                fx_matmul(t - 3)
+            if has(t + 1):
+                xm_turn(t + 1)
             if xs:
                 x_turn(xs)
+            if ends_head(t - 4):
+                spread((t - 4) // 2)
+            if ends_head(t - 7):
+                pool_matmul((t - 7) // 2)
+            if has(t - 3):
+                mass_sum(t - 3)
             if has(t):
                 row_max(t)
-            if has(t - 1):
-                row_inverse(t - 1)
-            if ends_head(t - 7):
-                store((t - 7) // 2)
+            if has(t - 3):
+                fx_bias(t - 3)
+            if has(t + 1):
+                xm_copy(t + 1)
+            if xs:
+                x_copy(xs)
             if ends_head(t - 3):
                 mass_add((t - 3) // 2)
             if has(t):
                 row_shift(t)
+            if has(t):
                 exps(t)
-            if has(t + 2):
-                xm_copy(t + 2)
-            if xs:
-                x_copy(xs)
+            if ends_head(t - 8):
+                store((t - 8) // 2)
             if has(t - 1):
                 scale_rows(t - 1)
+            if has(t - 1):
                 point_sum(t - 1)
-            if 0 <= t < H:
-                wfx_copy(t)
-            for v in xq:
-                x_quantise(v)
-            if has(t - 5):
-                fx_bias(t - 5)
-            if 0 <= t < H:
-                wfx_quantise(t)
             if has(t - 5):
                 normed(t - 5)
-                quantise("fx", t - 5)
+            if has(t - 3):
+                quantise('fx', t - 3)
+            if has(t - 5):
+                quantise('normed', t - 5)
             if ends_head(t - 3):
                 mass_inverse((t - 3) // 2)
-            if has(t - 5):
-                quantise("normed", t - 5)
+            if has(t - 0):
+                row_inverse(t - 0)

@@ -20,7 +20,8 @@ GROUPS_PER_BATCH = N // GROUP
 UNITS_PER_BATCH = H * GROUPS_PER_BATCH
 UNITS = B * UNITS_PER_BATCH
 XUNITS_PER_BATCH = GROUPS_PER_BATCH * PACK
-MASS_N = 128
+MASS_N = 96
+WARM_START = 5
 
 FLOPS = 2 * B * N * C * H * D + 2 * B * N * H * D * S + 2 * B * H * S * N * D
 
@@ -61,13 +62,13 @@ def tile_physicsattentionbase_pa_kernel(tc, x, x_mid, Wfx, bfx, Wslice, bslice, 
         xm_tiles = {}
         x_tiles = {}
         xm_tiles[0] = load_group(xm_rows, 0, "xm_sb")
+        xm_tiles[1] = load_group(xm_rows, 1, "xm_sb")
+        x_tiles[0] = load_group(x_rows, 0, "x_sb")
         wfx_raw = consts.tile([P, PACK, H * D], BF16)
         nc.sync.dma_start(
             out=wfx_raw[:].rearrange("q (u e) n -> q u (e n)", u=2),
             in_=Wfx.rearrange("(u q e) n -> q u (e n)", u=2, e=2),
         )
-        x_tiles[0] = load_group(x_rows, 0, "x_sb")
-        xm_tiles[1] = load_group(xm_rows, 1, "xm_sb")
         x_tiles[1] = load_group(x_rows, 1, "x_sb")
         bfx_bc = consts.tile([P, H * D], BF16)
         nc.sync.dma_start(out=bfx_bc[:], in_=bfx.partition_broadcast(P))
@@ -91,6 +92,14 @@ def tile_physicsattentionbase_pa_kernel(tc, x, x_mid, Wfx, bfx, Wslice, bslice, 
         nc.vector.reciprocal(out=inv_temp[:], in_=temp_bc[:])
         neg_inv_temp = consts.tile([P, H], F32)
         nc.vector.tensor_scalar_mul(out=neg_inv_temp[:], in0=inv_temp[:], scalar1=-1.0)
+
+        def warm_pass(n):
+            ps = one_ps.tile([P, PACK, D], F32, name="fx_ps")
+            for i in range(n):
+                nc.tensor.matmul(ps[:, 0, :], lhsT=ident_f32[:], rhs=ident_f32[:], start=True, stop=True)
+
+        if WARM_START:
+            warm_pass(WARM_START)
 
         wfx_grouped = consts.tile([P, H * D, PACK], BF16, align_bytes=64)
         wfx_codes = consts.tile([P, H * D], U32, align_bytes=64)
@@ -321,7 +330,7 @@ def tile_physicsattentionbase_pa_kernel(tc, x, x_mid, Wfx, bfx, Wslice, bslice, 
             nc.sync.dma_start(out=out[b, h], in_=sb[:])
 
         x_plan = {}
-        v, t = 0, -1
+        v, t = 0, 0
         while v < B * XUNITS_PER_BATCH:
             n = 2 if v < 8 else 1
             x_plan[t] = list(range(v, min(v + n, B * XUNITS_PER_BATCH)))
@@ -336,16 +345,12 @@ def tile_physicsattentionbase_pa_kernel(tc, x, x_mid, Wfx, bfx, Wslice, bslice, 
 
         for t in range(-4, UNITS + 12):
             xs = x_plan.get(t, [])
-            if 0 <= t + 2 < H:
-                wfx_copy(t + 2)
-            if 0 <= t + 2 < H:
-                wfx_quantise(t + 2)
             if has(t):
                 logits(t)
             for v in x_plan.get(t - 1, []):
                 x_quantise(v)
-            if has(t - 3):
-                fx_matmul(t - 3)
+            if has(t - 4):
+                fx_matmul(t - 4)
             if has(t + 1):
                 xm_turn(t + 1)
             if xs:
@@ -356,20 +361,24 @@ def tile_physicsattentionbase_pa_kernel(tc, x, x_mid, Wfx, bfx, Wslice, bslice, 
                 pool_matmul((t - 7) // 2)
             if has(t - 3):
                 mass_sum(t - 3)
-            if has(t):
-                row_max(t)
-            if has(t - 3):
-                fx_bias(t - 3)
+            if has(t - 0):
+                row_max(t - 0)
+            if 0 <= t + 0 < H:
+                wfx_copy(t + 0)
+            if has(t - 4):
+                fx_bias(t - 4)
+            if 0 <= t + 0 < H:
+                wfx_quantise(t + 0)
             if has(t + 1):
                 xm_copy(t + 1)
             if xs:
                 x_copy(xs)
             if ends_head(t - 3):
                 mass_add((t - 3) // 2)
-            if has(t):
-                row_shift(t)
-            if has(t):
-                exps(t)
+            if has(t - 0):
+                row_shift(t - 0)
+            if has(t - 0):
+                exps(t - 0)
             if ends_head(t - 8):
                 store((t - 8) // 2)
             if has(t - 1):
@@ -378,8 +387,8 @@ def tile_physicsattentionbase_pa_kernel(tc, x, x_mid, Wfx, bfx, Wslice, bslice, 
                 point_sum(t - 1)
             if has(t - 5):
                 normed(t - 5)
-            if has(t - 3):
-                quantise('fx', t - 3)
+            if has(t - 4):
+                quantise('fx', t - 4)
             if has(t - 5):
                 quantise('normed', t - 5)
             if ends_head(t - 3):

@@ -21,6 +21,7 @@ UNITS_PER_BATCH = H * GROUPS_PER_BATCH
 UNITS = B * UNITS_PER_BATCH
 XUNITS_PER_BATCH = GROUPS_PER_BATCH * PACK
 MASS_N = 96
+RUN = 4
 WARM_START = 5
 
 FLOPS = 2 * B * N * C * H * D + 2 * B * N * H * D * S + 2 * B * H * S * N * D
@@ -262,9 +263,12 @@ def tile_physicsattentionbase_pa_kernel(tc, x, x_mid, Wfx, bfx, Wslice, bslice, 
             b, h, i, g = place(u)
             grouped = work.tile([P, S, PACK], BF16, align_bytes=64, name="normed_grouped")
             nc.vector.tensor_tensor(
-                out=grouped[:],
-                in0=st["ws", u][:].rearrange("p j s -> p s j"),
-                in1=st["spread", u // 2][:].unsqueeze(2).to_broadcast([P, S, PACK]),
+                out=grouped[:].rearrange("p (c i) j -> p c j i", i=RUN),
+                in0=st["ws", u][:].rearrange("p j (c i) -> p c j i", i=RUN),
+                in1=st["spread", u // 2][:]
+                .rearrange("p (c i) -> p c i", i=RUN)
+                .unsqueeze(2)
+                .to_broadcast([P, S // RUN, PACK, RUN]),
                 op=ALU.mult,
             )
             st["normed", u] = grouped

@@ -150,11 +150,11 @@ def tile_physicsattentionbase_pa_kernel(tc, x, x_mid, Wfx, bfx, Wslice, bslice, 
                     nc.tensor.transpose(ps[:, n, e, :], words[:, col : col + P], ident_f32[:])
             st["xT_ps", vs[0]] = ps
 
-        def x_copy(vs):
+        def x_copy(vs, copy):
             ps = st["xT_ps", vs[0]]
             for n, v in enumerate(vs):
-                grouped = work.tile([P, P * PACK], BF16, align_bytes=64, name="x_grouped")
-                nc.scalar.copy(
+                grouped = work.tile([P, P * PACK], BF16, align_bytes=64, name="x_grouped", bufs=4)
+                copy(
                     out=grouped[:].bitcast(F32).rearrange("q (p u) -> q p u", u=2),
                     in_=ps[:, n, :, :].rearrange("q u p -> q p u"),
                 )
@@ -351,8 +351,6 @@ def tile_physicsattentionbase_pa_kernel(tc, x, x_mid, Wfx, bfx, Wslice, bslice, 
             xs = x_plan.get(t, [])
             if has(t):
                 logits(t)
-            for v in x_plan.get(t - 1, []):
-                x_quantise(v)
             if has(t - 4):
                 fx_matmul(t - 4)
             if has(t + 1):
@@ -365,18 +363,24 @@ def tile_physicsattentionbase_pa_kernel(tc, x, x_mid, Wfx, bfx, Wslice, bslice, 
                 pool_matmul((t - 7) // 2)
             if has(t - 3):
                 mass_sum(t - 3)
+            if 0 <= t < 4:
+                warm_pass(2)
             if has(t - 0):
                 row_max(t - 0)
+            if has(t - 1):
+                row_inverse(t - 1)
             if 0 <= t + 0 < H:
                 wfx_copy(t + 0)
             if has(t - 4):
                 fx_bias(t - 4)
+            if xs and xs[0] < 8:
+                x_copy(xs, nc.vector.tensor_copy)
             if 0 <= t + 0 < H:
                 wfx_quantise(t + 0)
             if has(t + 1):
                 xm_copy(t + 1)
-            if xs:
-                x_copy(xs)
+            if xs and xs[0] >= 8:
+                x_copy(xs, nc.scalar.copy)
             if ends_head(t - 3):
                 mass_add((t - 3) // 2)
             if has(t - 0):
@@ -391,11 +395,11 @@ def tile_physicsattentionbase_pa_kernel(tc, x, x_mid, Wfx, bfx, Wslice, bslice, 
                 point_sum(t - 1)
             if has(t - 5):
                 normed(t - 5)
+            for v in x_plan.get(t - 1, []):
+                x_quantise(v)
             if has(t - 4):
                 quantise('fx', t - 4)
-            if has(t - 5):
-                quantise('normed', t - 5)
             if ends_head(t - 3):
                 mass_inverse((t - 3) // 2)
-            if has(t - 0):
-                row_inverse(t - 0)
+            if has(t - 5):
+                quantise('normed', t - 5)

@@ -22,6 +22,7 @@ UNITS = B * UNITS_PER_BATCH
 XUNITS_PER_BATCH = GROUPS_PER_BATCH * PACK
 MASS_N = 96
 RUN = 4
+GS = 32
 WARM_START = 5
 
 FLOPS = 2 * B * N * C * H * D + 2 * B * N * H * D * S + 2 * B * H * S * N * D
@@ -259,18 +260,27 @@ def tile_physicsattentionbase_pa_kernel(tc, x, x_mid, Wfx, bfx, Wslice, bslice, 
             nc.tensor.transpose(ps[:], st["minv", k][:].to_broadcast([P, P]), ident_f32[:])
             st["spread", k] = ps
 
+        def spread_copy(k):
+            sb = small.tile([P, GS], F32, name="spread_sb")
+            nc.scalar.copy(out=sb[:], in_=st["spread", k][:, 0:GS])
+            st["spread_sb", k] = sb
+
         def normed(u):
             b, h, i, g = place(u)
             grouped = work.tile([P, S, PACK], BF16, align_bytes=64, name="normed_grouped")
-            nc.vector.tensor_tensor(
-                out=grouped[:].rearrange("p (c i) j -> p c j i", i=RUN),
-                in0=st["ws", u][:].rearrange("p j (c i) -> p c j i", i=RUN),
-                in1=st["spread", u // 2][:]
-                .rearrange("p (c i) -> p c i", i=RUN)
-                .unsqueeze(2)
-                .to_broadcast([P, S // RUN, PACK, RUN]),
-                op=ALU.mult,
-            )
+            for engine, factor, lo, hi in (
+                (nc.gpsimd, st["spread_sb", u // 2], 0, GS),
+                (nc.vector, st["spread", u // 2], GS, S),
+            ):
+                engine.tensor_tensor(
+                    out=grouped[:, lo:hi, :].rearrange("p (c i) j -> p c j i", i=RUN),
+                    in0=st["ws", u][:, :, lo:hi].rearrange("p j (c i) -> p c j i", i=RUN),
+                    in1=factor[:, lo:hi]
+                    .rearrange("p (c i) -> p c i", i=RUN)
+                    .unsqueeze(2)
+                    .to_broadcast([P, (hi - lo) // RUN, PACK, RUN]),
+                    op=ALU.mult,
+                )
             st["normed", u] = grouped
 
         def quantise(kind, u):
@@ -379,27 +389,29 @@ def tile_physicsattentionbase_pa_kernel(tc, x, x_mid, Wfx, bfx, Wslice, bslice, 
                 wfx_quantise(t + 0)
             if has(t + 1):
                 xm_copy(t + 1)
-            if xs and xs[0] >= 8:
-                x_copy(xs, nc.scalar.copy)
             if ends_head(t - 3):
                 mass_add((t - 3) // 2)
+            if ends_head(t - 4):
+                spread_copy((t - 4) // 2)
             if has(t - 0):
                 row_shift(t - 0)
+            if xs and xs[0] >= 8:
+                x_copy(xs, nc.scalar.copy)
             if has(t - 0):
                 exps(t - 0)
             if ends_head(t - 8):
                 store((t - 8) // 2)
+            if has(t - 5):
+                normed(t - 5)
             if has(t - 1):
                 scale_rows(t - 1)
             if has(t - 1):
                 point_sum(t - 1)
-            if has(t - 5):
-                normed(t - 5)
+            if has(t - 6):
+                quantise('normed', t - 6)
             for v in x_plan.get(t - 1, []):
                 x_quantise(v)
             if has(t - 4):
                 quantise('fx', t - 4)
             if ends_head(t - 3):
                 mass_inverse((t - 3) // 2)
-            if has(t - 5):
-                quantise('normed', t - 5)

@@ -20,8 +20,9 @@ GROUPS_PER_BATCH = N // GROUP
 UNITS_PER_BATCH = H * GROUPS_PER_BATCH
 UNITS = B * UNITS_PER_BATCH
 XUNITS_PER_BATCH = GROUPS_PER_BATCH * PACK
-MASS_N = 96
+MASS_N = 64
 RUN = 4
+FIRST_HEADS = 2
 GS = 32
 WARM_START = 5
 
@@ -54,6 +55,14 @@ def tile_physicsattentionbase_pa_kernel(tc, x, x_mid, Wfx, bfx, Wslice, bslice, 
             )
             return tile_sb
 
+        def load_heads(g, lo, hi, name):
+            tile_sb = inputs.tile([P, PACK, (hi - lo) * D], BF16, name=name, bufs=GROUPS_PER_BATCH)
+            nc.sync.dma_start(
+                out=tile_sb[:],
+                in_=xm_rows[g * GROUP : (g + 1) * GROUP, lo * D : hi * D].rearrange("(p j) c -> p j c", j=PACK),
+            )
+            return tile_sb
+
         wslice_sb = consts.tile([P, S], BF16)
         nc.scalar.dma_start(out=wslice_sb[:], in_=Wslice)
         bslice_col = consts.tile([P, 1], BF16)
@@ -63,8 +72,7 @@ def tile_physicsattentionbase_pa_kernel(tc, x, x_mid, Wfx, bfx, Wslice, bslice, 
 
         xm_tiles = {}
         x_tiles = {}
-        xm_tiles[0] = load_group(xm_rows, 0, "xm_sb")
-        xm_tiles[1] = load_group(xm_rows, 1, "xm_sb")
+        xm_first = [load_heads(g, 0, FIRST_HEADS, "xm_first") for g in range(GROUPS_PER_BATCH)]
         x_tiles[0] = load_group(x_rows, 0, "x_sb")
         wfx_raw = consts.tile([P, PACK, H * D], BF16)
         nc.sync.dma_start(
@@ -72,6 +80,7 @@ def tile_physicsattentionbase_pa_kernel(tc, x, x_mid, Wfx, bfx, Wslice, bslice, 
             in_=Wfx.rearrange("(u q e) n -> q u (e n)", u=2, e=2),
         )
         x_tiles[1] = load_group(x_rows, 1, "x_sb")
+        xm_rest = [load_heads(g, FIRST_HEADS, H, "xm_rest") for g in range(GROUPS_PER_BATCH)]
         bfx_bc = consts.tile([P, H * D], BF16)
         nc.sync.dma_start(out=bfx_bc[:], in_=bfx.partition_broadcast(P))
         for g in range(2, B * GROUPS_PER_BATCH):
@@ -132,8 +141,13 @@ def tile_physicsattentionbase_pa_kernel(tc, x, x_mid, Wfx, bfx, Wslice, bslice, 
             b, h, i, g = place(u)
             ps = one_ps.tile([P, PACK, P], BF16, name="xmT_ps")
             for j in range(PACK):
-                col = (j * H + h) * D
-                nc.tensor.transpose(ps[:, j, :], xm_tiles[g][:, col : col + D], ident_bf16[:])
+                if g >= GROUPS_PER_BATCH:
+                    points = xm_tiles[g][:, (j * H + h) * D : (j * H + h + 1) * D]
+                elif h < FIRST_HEADS:
+                    points = xm_first[g][:, j, h * D : (h + 1) * D]
+                else:
+                    points = xm_rest[g][:, j, (h - FIRST_HEADS) * D : (h - FIRST_HEADS + 1) * D]
+                nc.tensor.transpose(ps[:, j, :], points, ident_bf16[:])
             st["xmT_ps", u] = ps
 
         def xm_copy(u):
@@ -374,7 +388,7 @@ def tile_physicsattentionbase_pa_kernel(tc, x, x_mid, Wfx, bfx, Wslice, bslice, 
             if has(t - 3):
                 mass_sum(t - 3)
             if 0 <= t < 4:
-                warm_pass(2)
+                warm_pass(1)
             if has(t - 0):
                 row_max(t - 0)
             if has(t - 1):
@@ -411,7 +425,7 @@ def tile_physicsattentionbase_pa_kernel(tc, x, x_mid, Wfx, bfx, Wslice, bslice, 
                 quantise('normed', t - 6)
             for v in x_plan.get(t - 1, []):
                 x_quantise(v)
-            if has(t - 4):
-                quantise('fx', t - 4)
             if ends_head(t - 3):
                 mass_inverse((t - 3) // 2)
+            if has(t - 4):
+                quantise('fx', t - 4)

from contextlib import ExitStack

import concourse.mybir as mybir
from concourse.masks import make_identity

F32 = mybir.dt.float32
BF16 = mybir.dt.bfloat16
U32 = mybir.dt.uint32
U8 = mybir.dt.uint8
FP8X4 = mybir.dt.float8_e4m3fn_x4
ALU = mybir.AluOpType
ACT = mybir.ActivationFunctionType
AXIS = mybir.AxisListType

B, N, C, H, D, S = 4, 1024, 512, 4, 128, 128
P = 128
PACK = 4
GROUP = P * PACK
GROUPS_PER_BATCH = N // GROUP
UNITS_PER_BATCH = H * GROUPS_PER_BATCH
UNITS = B * UNITS_PER_BATCH
XUNITS_PER_BATCH = GROUPS_PER_BATCH * PACK
MASS_N = 64
RUN = 4
FIRST_HEADS = 2
GS = 32
WARM_START = 5

FLOPS = 2 * B * N * C * H * D + 2 * B * N * H * D * S + 2 * B * H * S * N * D


def tile_physicsattentionbase_pa_kernel(tc, x, x_mid, Wfx, bfx, Wslice, bslice, temp, out):
    nc = tc.nc
    x_rows = x.rearrange("b n c -> (b n) c")
    xm_rows = x_mid.rearrange("b n h d -> (b n) (h d)")

    with ExitStack() as ctx:
        consts = ctx.enter_context(tc.tile_pool(name="consts", bufs=1))
        inputs = ctx.enter_context(tc.tile_pool(name="inputs", bufs=B * GROUPS_PER_BATCH))
        work = ctx.enter_context(tc.tile_pool(name="work", bufs=3))
        wide = ctx.enter_context(tc.tile_pool(name="wide", bufs=7))
        packed = ctx.enter_context(tc.tile_pool(name="packed", bufs=6))
        xpacked = ctx.enter_context(tc.tile_pool(name="xpacked", bufs=2 * XUNITS_PER_BATCH + 4))
        small = ctx.enter_context(tc.tile_pool(name="small", bufs=6))
        z_pool = ctx.enter_context(tc.psum_pool(name="z_pool", bufs=2))
        one_ps = ctx.enter_context(tc.psum_pool(name="one_ps", bufs=1))

        ctx.enter_context(tc.manual_schedule())

        def load_group(rows, g, name):
            tile_sb = inputs.tile([P, PACK * C], BF16, name=name)
            nc.sync.dma_start(
                out=tile_sb[:],
                in_=rows[g * GROUP : (g + 1) * GROUP, :].rearrange("(p j) c -> p (j c)", j=PACK),
            )
            return tile_sb

        def load_heads(g, lo, hi, name):
            tile_sb = inputs.tile([P, PACK, (hi - lo) * D], BF16, name=name, bufs=GROUPS_PER_BATCH)
            nc.sync.dma_start(
                out=tile_sb[:],
                in_=xm_rows[g * GROUP : (g + 1) * GROUP, lo * D : hi * D].rearrange("(p j) c -> p j c", j=PACK),
            )
            return tile_sb

        wslice_sb = consts.tile([P, S], BF16)
        nc.scalar.dma_start(out=wslice_sb[:], in_=Wslice)
        bslice_col = consts.tile([P, 1], BF16)
        nc.scalar.dma_start(out=bslice_col[:], in_=bslice.rearrange("(s o) -> s o", o=1))
        temp_bc = consts.tile([P, H], BF16)
        nc.scalar.dma_start(out=temp_bc[:], in_=temp.rearrange("a b h c -> (a b h c)").partition_broadcast(P))

        xm_tiles = {}
        x_tiles = {}
        xm_first = [load_heads(g, 0, FIRST_HEADS, "xm_first") for g in range(GROUPS_PER_BATCH)]
        x_tiles[0] = load_group(x_rows, 0, "x_sb")
        wfx_raw = consts.tile([P, PACK, H * D], BF16)
        nc.sync.dma_start(
            out=wfx_raw[:].rearrange("q (u e) n -> q u (e n)", u=2),
            in_=Wfx.rearrange("(u q e) n -> q u (e n)", u=2, e=2),
        )
        x_tiles[1] = load_group(x_rows, 1, "x_sb")
        xm_rest = [load_heads(g, FIRST_HEADS, H, "xm_rest") for g in range(GROUPS_PER_BATCH)]
        bfx_bc = consts.tile([P, H * D], BF16)
        nc.sync.dma_start(out=bfx_bc[:], in_=bfx.partition_broadcast(P))
        for g in range(2, B * GROUPS_PER_BATCH):
            xm_tiles[g] = load_group(xm_rows, g, "xm_sb")
            x_tiles[g] = load_group(x_rows, g, "x_sb")

        ident_bf16 = consts.tile([P, P], BF16)
        make_identity(nc, ident_bf16[:])
        ident_f32 = consts.tile([P, P], F32)
        make_identity(nc, ident_f32[:])
        ones_f32 = consts.tile([P, MASS_N], F32)
        nc.gpsimd.memset(ones_f32[:], 1.0)
        zero_col = consts.tile([P, 1], F32)
        nc.vector.memset(zero_col[:], 0.0)
        warm_col = consts.tile([P, 1], F32)
        nc.scalar.activation(out=warm_col[:], in_=zero_col[:], func=ACT.Exp)
        bslice_rep = consts.tile([P, P], F32)
        nc.vector.tensor_copy(out=bslice_rep[:], in_=bslice_col[:].to_broadcast([P, P]))
        inv_temp = consts.tile([P, H], F32)
        nc.vector.reciprocal(out=inv_temp[:], in_=temp_bc[:])
        neg_inv_temp = consts.tile([P, H], F32)
        nc.vector.tensor_scalar_mul(out=neg_inv_temp[:], in0=inv_temp[:], scalar1=-1.0)

        def warm_pass(n):
            ps = one_ps.tile([P, PACK, D], F32, name="fx_ps")
            for i in range(n):
                nc.tensor.matmul(ps[:, 0, :], lhsT=ident_f32[:], rhs=ident_f32[:], start=True, stop=True)

        if WARM_START:
            warm_pass(WARM_START)

        wfx_grouped = consts.tile([P, H * D, PACK], BF16, align_bytes=64)
        wfx_codes = consts.tile([P, H * D], U32, align_bytes=64)
        wfx_scales = consts.tile([P, H * D], U8, align_bytes=64)

        def wfx_copy(h):
            cols = slice(h * D, (h + 1) * D)
            nc.vector.tensor_copy(out=wfx_grouped[:, cols, :], in_=wfx_raw[:, :, cols].rearrange("q t n -> q n t"))
            st["wc", h] = 1

        def wfx_quantise(h):
            st["wq", h] = st["wc", h]
            cols = slice(h * D, (h + 1) * D)
            nc.vector.quantize_mx(
                out=wfx_codes[:, cols].bitcast(FP8X4),
                scales=wfx_scales[:, cols],
                in_=wfx_grouped[:, cols, :].rearrange("q n t -> q (n t)"),
            )

        def place(u):
            b, r = divmod(u, UNITS_PER_BATCH)
            h, i = divmod(r, GROUPS_PER_BATCH)
            return b, h, i, b * GROUPS_PER_BATCH + i

        st = {}

        def xm_turn(u):
            b, h, i, g = place(u)
            ps = one_ps.tile([P, PACK, P], BF16, name="xmT_ps")
            for j in range(PACK):
                if g >= GROUPS_PER_BATCH:
                    points = xm_tiles[g][:, (j * H + h) * D : (j * H + h + 1) * D]
                elif h < FIRST_HEADS:
                    points = xm_first[g][:, j, h * D : (h + 1) * D]
                else:
                    points = xm_rest[g][:, j, (h - FIRST_HEADS) * D : (h - FIRST_HEADS + 1) * D]
                nc.tensor.transpose(ps[:, j, :], points, ident_bf16[:])
            st["xmT_ps", u] = ps

        def xm_copy(u):
            sb = work.tile([P, PACK, P], BF16, name="xmT_sb")
            nc.scalar.copy(out=sb[:], in_=st["xmT_ps", u][:])
            st["xmT", u] = sb

        def x_turn(vs):
            ps = one_ps.tile([P, 2, 2, P], F32, name="xT_ps")
            for n, v in enumerate(vs):
                g, j = divmod(v, PACK)
                words = x_tiles[g][:].bitcast(F32)
                for e in range(2):
                    col = (j * 2 + e) * P
                    nc.tensor.transpose(ps[:, n, e, :], words[:, col : col + P], ident_f32[:])
            st["xT_ps", vs[0]] = ps

        def x_copy(vs, copy):
            ps = st["xT_ps", vs[0]]
            for n, v in enumerate(vs):
                grouped = work.tile([P, P * PACK], BF16, align_bytes=64, name="x_grouped", bufs=4)
                copy(
                    out=grouped[:].bitcast(F32).rearrange("q (p u) -> q p u", u=2),
                    in_=ps[:, n, :, :].rearrange("q u p -> q p u"),
                )
                st["x_grouped", v] = grouped

        def x_quantise(v):
            codes = xpacked.tile([P, P], U32, align_bytes=64, name="x_codes")
            scales = xpacked.tile([P, P], U8, align_bytes=64, name="x_scales")
            nc.vector.quantize_mx(
                out=codes[:].bitcast(FP8X4), scales=scales[:], in_=st["x_grouped", v][:]
            )
            st["x_ops", v] = (codes, scales)

        def logits(u):
            xmT = st["xmT", u]
            ps = z_pool.tile([P, PACK, S], F32, name="z_ps")
            for j in range(PACK):
                nc.tensor.matmul(
                    ps[:, j, :], lhsT=bslice_rep[:], rhs=ident_f32[:], is_transpose=True, start=(j == 0), stop=False
                )
            for j in range(PACK):
                nc.tensor.matmul(
                    ps[:, j, :], lhsT=xmT[:, j, :], rhs=wslice_sb[:], start=False, stop=(j == PACK - 1)
                )
            st["z", u] = ps

        def row_max(u):
            m = small.tile([P, PACK], F32, name="row_max")
            nc.vector.tensor_reduce(out=m[:], in_=st["z", u][:], axis=AXIS.X, op=ALU.max)
            st["max", u] = m

        def row_shift(u):
            b, h, i, g = place(u)
            shift = small.tile([P, PACK], F32, name="shift")
            nc.scalar.activation(
                out=shift[:], in_=st["max", u][:], func=ACT.Copy, scale=neg_inv_temp[:, h : h + 1]
            )
            st["shift", u] = shift

        def exps(u):
            b, h, i, g = place(u)
            ps, shift = st["z", u], st["shift", u]
            w = wide.tile([P, PACK, S], F32, name="w_sb")
            row_sum = small.tile([P, PACK], F32, name="row_sum")
            for j in range(PACK):
                nc.scalar.activation(
                    out=w[:, j, :],
                    in_=ps[:, j, :],
                    func=ACT.Exp,
                    bias=shift[:, j : j + 1],
                    scale=inv_temp[:, h : h + 1],
                    accum_out=row_sum[:, j : j + 1],
                )
            st["w", u] = w
            st["sum", u] = row_sum

        def row_inverse(u):
            r = small.tile([P, PACK], F32, name="row_inv")
            nc.vector.reciprocal(out=r[:], in_=st["sum", u][:])
            st["inv", u] = r

        def scale_rows(u):
            w, r = st["w", u], st["inv", u]
            for j in range(PACK):
                nc.scalar.activation(out=w[:, j, :], in_=w[:, j, :], func=ACT.Copy, scale=r[:, j : j + 1])
            st["ws", u] = w

        def point_sum(u):
            w = st["ws", u]
            pair = small.tile([P, 2, S], F32, name="pair")
            nc.gpsimd.tensor_tensor(out=pair[:], in0=w[:, 0:2, :], in1=w[:, 2:4, :], op=ALU.add)
            tot = small.tile([P, S], F32, name="tot")
            nc.gpsimd.tensor_tensor(out=tot[:], in0=pair[:, 0, :], in1=pair[:, 1, :], op=ALU.add)
            st["tot", u] = tot

        def mass_sum(u):
            b, h, i, g = place(u)
            if i == 0:
                st["mass", u // 2] = one_ps.tile([P, MASS_N], F32, name="mass_ps")
            nc.tensor.matmul(
                st["mass", u // 2][:],
                lhsT=st["tot", u][:],
                rhs=ones_f32[:],
                start=(i == 0),
                stop=(i == GROUPS_PER_BATCH - 1),
            )
            if i == GROUPS_PER_BATCH - 1:
                st["mass_done", u // 2] = st["mass", u // 2]

        def mass_add(k):
            m = small.tile([P, 1], F32, name="mass")
            nc.scalar.activation(out=m[:], in_=st["mass_done", k][:, 0:1], func=ACT.Copy, bias=0.01)
            st["mass1", k] = m

        def mass_inverse(k):
            r = small.tile([P, 1], F32, name="inv_mass")
            nc.vector.reciprocal(out=r[:], in_=st["mass1", k][:])
            st["minv", k] = r

        def spread(k):
            ps = one_ps.tile([P, S], F32, name="inv_mass_ps")
            nc.tensor.transpose(ps[:], st["minv", k][:].to_broadcast([P, P]), ident_f32[:])
            st["spread", k] = ps

        def spread_copy(k):
            sb = small.tile([P, GS], F32, name="spread_sb")
            nc.scalar.copy(out=sb[:], in_=st["spread", k][:, 0:GS])
            st["spread_sb", k] = sb

        def normed(u):
            b, h, i, g = place(u)
            grouped = work.tile([P, S, PACK], BF16, align_bytes=64, name="normed_grouped")
            for engine, factor, lo, hi in (
                (nc.gpsimd, st["spread_sb", u // 2], 0, GS),
                (nc.vector, st["spread", u // 2], GS, S),
            ):
                engine.tensor_tensor(
                    out=grouped[:, lo:hi, :].rearrange("p (c i) j -> p c j i", i=RUN),
                    in0=st["ws", u][:, :, lo:hi].rearrange("p j (c i) -> p c j i", i=RUN),
                    in1=factor[:, lo:hi]
                    .rearrange("p (c i) -> p c i", i=RUN)
                    .unsqueeze(2)
                    .to_broadcast([P, (hi - lo) // RUN, PACK, RUN]),
                    op=ALU.mult,
                )
            st["normed", u] = grouped

        def quantise(kind, u):
            grouped = st[kind, u]
            codes = packed.tile([P, P], U32, align_bytes=64, name=kind + "_codes")
            scales = packed.tile([P, P], U8, align_bytes=64, name=kind + "_scales")
            nc.vector.quantize_mx(
                out=codes[:].bitcast(FP8X4), scales=scales[:], in_=grouped[:].rearrange("p s j -> p (s j)")
            )
            st[kind + "_ops", u] = (codes, scales)

        def fx_matmul(u):
            b, h, i, g = place(u)
            assert st["wq", h]
            ps = one_ps.tile([P, PACK, D], F32, name="fx_ps")
            cols = slice(h * D, (h + 1) * D)
            for j in range(PACK):
                x_codes, x_scales = st["x_ops", g * PACK + j]
                nc.tensor.matmul_mx(
                    out=ps[:, j, :],
                    lhsT=x_codes[:].bitcast(FP8X4),
                    lhsT_scale=x_scales[:],
                    rhs=wfx_codes[:, cols].bitcast(FP8X4),
                    rhs_scale=wfx_scales[:, cols],
                    start=True,
                    stop=True,
                )
            st["fx_ps", u] = ps

        def fx_bias(u):
            b, h, i, g = place(u)
            grouped = work.tile([P, D, PACK], BF16, align_bytes=64, name="fx_grouped")
            nc.vector.tensor_tensor(
                out=grouped[:],
                in0=st["fx_ps", u][:].rearrange("p j d -> p d j"),
                in1=bfx_bc[:, h * D : (h + 1) * D].unsqueeze(2).to_broadcast([P, D, PACK]),
                op=ALU.add,
            )
            st["fx", u] = grouped

        def pool_matmul(k):
            ps = one_ps.tile([P, D], F32, name="out_ps")
            for i in range(GROUPS_PER_BATCH):
                n_codes, n_scales = st["normed_ops", 2 * k + i]
                f_codes, f_scales = st["fx_ops", 2 * k + i]
                nc.tensor.matmul_mx(
                    out=ps[:],
                    lhsT=n_codes[:].bitcast(FP8X4),
                    lhsT_scale=n_scales[:],
                    rhs=f_codes[:].bitcast(FP8X4),
                    rhs_scale=f_scales[:],
                    start=(i == 0),
                    stop=(i == GROUPS_PER_BATCH - 1),
                )
            st["out_ps", k] = ps

        def store(k):
            b, h = divmod(k, H)
            sb = work.tile([P, D], F32, name="out_sb")
            nc.scalar.copy(out=sb[:], in_=st["out_ps", k][:])
            nc.sync.dma_start(out=out[b, h], in_=sb[:])

        x_plan = {}
        v, t = 0, 0
        while v < B * XUNITS_PER_BATCH:
            n = 2 if v < 8 else 1
            x_plan[t] = list(range(v, min(v + n, B * XUNITS_PER_BATCH)))
            v += n
            t += 1

        def has(u):
            return 0 <= u < UNITS

        def ends_head(u):
            return has(u) and u % GROUPS_PER_BATCH == GROUPS_PER_BATCH - 1

        for t in range(-4, UNITS + 12):
            xs = x_plan.get(t, [])
            if has(t):
                logits(t)
            if has(t - 4):
                fx_matmul(t - 4)
            if has(t + 1):
                xm_turn(t + 1)
            if xs:
                x_turn(xs)
            if ends_head(t - 4):
                spread((t - 4) // 2)
            if ends_head(t - 7):
                pool_matmul((t - 7) // 2)
            if has(t - 3):
                mass_sum(t - 3)
            if 0 <= t < 4:
                warm_pass(1)
            if has(t - 0):
                row_max(t - 0)
            if has(t - 1):
                row_inverse(t - 1)
            if 0 <= t + 0 < H:
                wfx_copy(t + 0)
            if has(t - 4):
                fx_bias(t - 4)
            if xs and xs[0] < 8:
                x_copy(xs, nc.vector.tensor_copy)
            if 0 <= t + 0 < H:
                wfx_quantise(t + 0)
            if has(t + 1):
                xm_copy(t + 1)
            if ends_head(t - 3):
                mass_add((t - 3) // 2)
            if ends_head(t - 4):
                spread_copy((t - 4) // 2)
            if has(t - 0):
                row_shift(t - 0)
            if xs and xs[0] >= 8:
                x_copy(xs, nc.scalar.copy)
            if has(t - 0):
                exps(t - 0)
            if ends_head(t - 8):
                store((t - 8) // 2)
            if has(t - 5):
                normed(t - 5)
            if has(t - 1):
                scale_rows(t - 1)
            if has(t - 1):
                point_sum(t - 1)
            if has(t - 6):
                quantise('normed', t - 6)
            for v in x_plan.get(t - 1, []):
                x_quantise(v)
            if ends_head(t - 3):
                mass_inverse((t - 3) // 2)
            if has(t - 4):
                quantise('fx', t - 4)
